import numpy as np
import ml_dtypes


def mxq(x, axis, fmt="e4m3"):
    dtype, down = {"e4m3": (ml_dtypes.float8_e4m3fn, 7), "e5m2": (ml_dtypes.float8_e5m2, 14)}[fmt]
    v = np.moveaxis(np.asarray(x, np.float32).astype(ml_dtypes.bfloat16).astype(np.float64), axis, -1)
    blocks = v.reshape(v.shape[:-1] + (-1, 32))
    amax = np.abs(blocks).max(-1, keepdims=True)
    byte = np.maximum(np.where(amax > 0, np.frexp(amax)[1] - 1 + 127, 0) - down, 1)
    scale = np.exp2(byte - 127.0)
    codes = (blocks / scale).astype(np.float32).astype(dtype).astype(np.float64)
    return np.moveaxis((codes * scale).reshape(v.shape), -1, axis)


WIDE = False


def mx_kscale(k):
    if not WIDE:
        return np.ones(k)
    levels = np.array([10, -10, 5, -5, 0])
    a = np.random.permutation(np.resize(levels, k // 512 * 4)).reshape(k // 512, 4)
    idx = np.arange(k)
    return np.exp2(a[idx // 512, idx % 128 // 32])


BF16 = ml_dtypes.bfloat16


def bf(x):
    return np.asarray(x, np.float32).astype(BF16)


def f64(x):
    return np.asarray(x).astype(np.float64)


E2M1 = np.array([0.0, 0.5, 1.0, 1.5, 2.0, 3.0, 4.0, 6.0, -0.0, -0.5, -1.0, -1.5, -2.0, -3.0, -4.0, -6.0])


def pack_weight(w, fmt):
    k, n = w.shape
    w = f64(bf(w)).reshape(k // 32, 32, n)
    amax = np.abs(w).max(1)
    if fmt == "e4m3":
        byte = np.frexp(amax)[1] - 1 + 127 - 7
    else:
        mant, ex = np.frexp(amax / 6.0)
        byte = np.where(mant > 0.5, ex, ex - 1) + 127
    byte = np.clip(np.where(amax > 0, byte, 1), 1, 254)
    scaled = (w * np.exp2(127.0 - byte)[:, None, :]).reshape(k, n).astype(np.float32)
    by_word = np.ascontiguousarray(scaled.reshape(k // 512, 128, 4, n).transpose(0, 1, 3, 2))
    if fmt == "e4m3":
        words = by_word.astype(ml_dtypes.float8_e4m3fn).view(np.uint8)
    else:
        c = by_word.astype(ml_dtypes.float4_e2m1fn).view(np.uint8) & 0xF
        words = c[..., 0::2] | (c[..., 1::2] << 4)
    return np.ascontiguousarray(words), np.ascontiguousarray(byte.astype(np.uint8).reshape(k // 512, 16, n))


def unpack_weight(words, scales, fmt):
    g, p, n, _ = words.shape
    if fmt == "e4m3":
        vals = np.ascontiguousarray(words).view(ml_dtypes.float8_e4m3fn).astype(np.float64)
    else:
        nib = np.empty((g, p, n, 4), np.uint8)
        nib[..., 0::2] = words & 0xF
        nib[..., 1::2] = words >> 4
        vals = E2M1[nib]
    vals = vals * np.repeat(np.exp2(scales.astype(np.float64) - 127.0), 8, axis=1)[..., None]
    return vals.transpose(0, 1, 3, 2).reshape(g * 512, n)


B, N, F, FO, KC = 32, 512, 128, 1024, 5


def setup_inputs():
    d = mx_kscale(N)
    d = d / d.max()
    a = np.random.standard_normal((N, N)) / np.sqrt(N)
    z0 = bf(np.random.standard_normal((B, N, F)) * d[:, None])
    z1 = bf(0.7 * np.random.standard_normal((B, N, F)) * d[:, None])
    lap = 0.5 * (a + a.T) * d[:, None] / d[None, :]
    words, scales = pack_weight(np.ascontiguousarray(lap.T), "e4m3")
    return {"z0": z0, "z1": z1, "L_words": words, "L_scales": scales}


def reference(z0, z1, L_words, L_scales):
    z0, z1 = f64(z0), f64(z1)
    lq = unpack_weight(L_words, L_scales, "e4m3").T
    z2 = 2.0 * (lq @ mxq(z1, 1, "e4m3")) - z0
    z3 = 2.0 * (lq @ mxq(z2, 1, "e4m3")) - z1
    return z2, z3

@@ -1,0 +1,158 @@
+from contextlib import ExitStack
+
+import concourse.mybir as mybir
+from concourse.masks import make_identity
+
+F32 = mybir.dt.float32
+BF16 = mybir.dt.bfloat16
+I32 = mybir.dt.int32
+U32 = mybir.dt.uint32
+U8 = mybir.dt.uint8
+FP8X4 = mybir.dt.float8_e4m3fn_x4
+MULT = mybir.AluOpType.mult
+SUBTRACT = mybir.AluOpType.subtract
+
+P = 128
+PACK = 4
+BATCH = 32
+NODES = P * PACK
+FEATS = 128
+CHUNK = 4
+N_CHUNKS = BATCH // CHUNK
+
+FLOPS = 2 * 2 * BATCH * NODES * NODES * FEATS
+
+
+def by_partition(dram, c):
+    return dram[c * CHUNK : (c + 1) * CHUNK].rearrange("b (p t) f -> p b (t f)", t=PACK)
+
+
+def tile_manualchebconv_pb_t_kernel(tc, z0, z1, L_words, L_scales, out_0, out_1):
+    nc = tc.nc
+    with ExitStack() as stack:
+        keep = stack.enter_context(tc.tile_pool(name="keep", bufs=1))
+        quant = stack.enter_context(tc.tile_pool(name="quant", bufs=2))
+        z1_mx = stack.enter_context(tc.tile_pool(name="z1_mx", bufs=3))
+        rows = stack.enter_context(tc.tile_pool(name="rows", bufs=2 * CHUNK))
+        results = stack.enter_context(tc.tile_pool(name="results", bufs=5))
+        sums_pool = stack.enter_context(tc.psum_pool(name="sums", bufs=CHUNK))
+        turned_pool = stack.enter_context(tc.psum_pool(name="turned", bufs=CHUNK))
+        stack.enter_context(tc.manual_schedule())
+
+        identity = keep.tile([P, P], F32)
+        make_identity(nc, identity[:])
+
+        w_words = keep.tile([P, NODES * PACK], U8, align_bytes=64)
+        w_scales = keep.tile([P, NODES], U8, align_bytes=64)
+        nc.vector.memset(w_scales[:].bitcast(I32), 0)
+
+        z0_tiles = [keep.tile([P, CHUNK, NODES], BF16, name="z0_%d" % c) for c in range(N_CHUNKS)]
+        z1_tiles = [keep.tile([P, CHUNK, NODES], BF16, name="z1_%d" % c) for c in range(N_CHUNKS)]
+
+        nc.sync.dma_start(out=z1_tiles[0][:], in_=by_partition(z1, 0))
+        scale_rows = L_scales.rearrange("g q n -> (g q) n")
+        for quadrant in range(4):
+            nc.sync.dma_start(
+                out=w_scales[32 * quadrant : 32 * quadrant + 4, :].bitcast(I32),
+                in_=scale_rows[4 * quadrant : 4 * quadrant + 4, :].bitcast(I32),
+            )
+        nc.sync.dma_start(
+            out=w_words[:].bitcast(I32),
+            in_=L_words.rearrange("g p n t -> (g p) (n t)").bitcast(I32),
+        )
+        nc.sync.dma_start(out=z0_tiles[0][:], in_=by_partition(z0, 0))
+        for c in range(1, N_CHUNKS):
+            nc.sync.dma_start(out=z1_tiles[c][:], in_=by_partition(z1, c))
+            nc.sync.dma_start(out=z0_tiles[c][:], in_=by_partition(z0, c))
+
+        def quantise(grouped, codes, scales):
+            nc.vector.quantize_mx(
+                out=codes[:].bitcast(FP8X4),
+                scales=scales[:],
+                in_=grouped[:].rearrange("p b f t -> p (b f t)"),
+            )
+
+        def multiply(codes, scales):
+            banks = []
+            for b in range(CHUNK):
+                sums = sums_pool.tile([P, NODES], F32)
+                cols = slice(b * FEATS, (b + 1) * FEATS)
+                nc.tensor.matmul_mx(
+                    out=sums[:],
+                    lhsT=codes[:, cols].bitcast(FP8X4),
+                    lhsT_scale=scales[:, cols],
+                    rhs=w_words[:].bitcast(FP8X4),
+                    rhs_scale=w_scales[:],
+                    start=True,
+                    stop=True,
+                )
+                banks.append(sums)
+            return banks
+
+        def copy_out(banks):
+            sorted_rows = []
+            for sums in banks:
+                by_feature = rows.tile([P, PACK, P], F32)
+                nc.scalar.copy(
+                    out=by_feature[:], in_=sums[:].rearrange("f (p t) -> f t p", t=PACK)
+                )
+                sorted_rows.append(by_feature)
+            return sorted_rows
+
+        def finish(sorted_rows, older, out, c):
+            result = results.tile([P, CHUNK, NODES], F32)
+            for b in range(CHUNK):
+                turned = turned_pool.tile([P, PACK, FEATS], F32)
+                for t in range(PACK):
+                    nc.tensor.transpose(
+                        out=turned[:, t, :], in_=sorted_rows[b][:, t, :], identity=identity[:]
+                    )
+                nc.vector.scalar_tensor_tensor(
+                    out=result[:, b, :],
+                    in0=turned[:].rearrange("p t f -> p (t f)"),
+                    scalar=2.0,
+                    in1=older[:, b, :],
+                    op0=MULT,
+                    op1=SUBTRACT,
+                )
+            nc.sync.dma_start(out=by_partition(out, c), in_=result[:])
+            return result
+
+        def regroup_z1(c):
+            grouped_z1 = quant.tile([P, CHUNK, FEATS, PACK], BF16, align_bytes=64)
+            nc.vector.tensor_copy(
+                out=grouped_z1[:], in_=z1_tiles[c][:].rearrange("p b (t f) -> p b f t", t=PACK)
+            )
+            return grouped_z1
+
+        def quantise_z1(grouped_z1):
+            z1_codes = z1_mx.tile([P, CHUNK * FEATS], U32, align_bytes=64)
+            z1_scales = z1_mx.tile([P, CHUNK * FEATS], U8, align_bytes=64)
+            quantise(grouped_z1, z1_codes, z1_scales)
+            return z1_codes, z1_scales
+
+        z1_ready = [quantise_z1(regroup_z1(0)), quantise_z1(regroup_z1(1))]
+        z2_ready = []
+        for c in range(N_CHUNKS):
+            z2 = finish(copy_out(multiply(*z1_ready[c])), z0_tiles[c], out_0, c)
+            grouped_z2 = quant.tile([P, CHUNK, FEATS, PACK], BF16, align_bytes=64)
+            for b in range(CHUNK):
+                nc.scalar.copy(
+                    out=grouped_z2[:, b, :, :],
+                    in_=z2[:, b, :].rearrange("p (t f) -> p f t", t=PACK),
+                )
+            if c + 2 < N_CHUNKS:
+                grouped_z1 = regroup_z1(c + 2)
+            z2_codes = keep.tile([P, CHUNK * FEATS], U32, name="z2_codes_%d" % c, align_bytes=64)
+            z2_scales = keep.tile([P, CHUNK * FEATS], U8, name="z2_scales_%d" % c, align_bytes=64)
+            quantise(grouped_z2, z2_codes, z2_scales)
+            z2_ready.append((z2_codes, z2_scales))
+            if c + 2 < N_CHUNKS:
+                z1_ready.append(quantise_z1(grouped_z1))
+
+        banks = multiply(*z2_ready[0])
+        for c in range(N_CHUNKS):
+            sorted_rows = copy_out(banks)
+            if c + 1 < N_CHUNKS:
+                banks = multiply(*z2_ready[c + 1])
+            finish(sorted_rows, z1_tiles[c], out_1, c)

@@ -19,6 +19,7 @@ NODES = P * PACK
 FEATS = 128
 CHUNK = 4
 N_CHUNKS = BATCH // CHUNK
+RUN = 4
 
 FLOPS = 2 * 2 * BATCH * NODES * NODES * FEATS
 
@@ -31,10 +32,11 @@ def tile_manualchebconv_pb_t_kernel(tc, z0, z1, L_words, L_scales, out_0, out_1)
     nc = tc.nc
     with ExitStack() as stack:
         keep = stack.enter_context(tc.tile_pool(name="keep", bufs=1))
-        quant = stack.enter_context(tc.tile_pool(name="quant", bufs=2))
+        z1_quant = stack.enter_context(tc.tile_pool(name="z1_quant", bufs=2))
+        z2_quant = stack.enter_context(tc.tile_pool(name="z2_quant", bufs=3))
         z1_mx = stack.enter_context(tc.tile_pool(name="z1_mx", bufs=3))
         rows = stack.enter_context(tc.tile_pool(name="rows", bufs=2 * CHUNK))
-        results = stack.enter_context(tc.tile_pool(name="results", bufs=5))
+        results = stack.enter_context(tc.tile_pool(name="results", bufs=7))
         sums_pool = stack.enter_context(tc.psum_pool(name="sums", bufs=CHUNK))
         turned_pool = stack.enter_context(tc.psum_pool(name="turned", bufs=CHUNK))
         stack.enter_context(tc.manual_schedule())
@@ -60,9 +62,9 @@ def tile_manualchebconv_pb_t_kernel(tc, z0, z1, L_words, L_scales, out_0, out_1)
             out=w_words[:].bitcast(I32),
             in_=L_words.rearrange("g p n t -> (g p) (n t)").bitcast(I32),
         )
-        nc.sync.dma_start(out=z0_tiles[0][:], in_=by_partition(z0, 0))
-        for c in range(1, N_CHUNKS):
-            nc.sync.dma_start(out=z1_tiles[c][:], in_=by_partition(z1, c))
+        for c in range(N_CHUNKS):
+            if c + 1 < N_CHUNKS:
+                nc.sync.dma_start(out=z1_tiles[c + 1][:], in_=by_partition(z1, c + 1))
             nc.sync.dma_start(out=z0_tiles[c][:], in_=by_partition(z0, c))
 
         def quantise(grouped, codes, scales):
@@ -119,9 +121,10 @@ def tile_manualchebconv_pb_t_kernel(tc, z0, z1, L_words, L_scales, out_0, out_1)
             return result
 
         def regroup_z1(c):
-            grouped_z1 = quant.tile([P, CHUNK, FEATS, PACK], BF16, align_bytes=64)
+            grouped_z1 = z1_quant.tile([P, CHUNK, FEATS, PACK], BF16, align_bytes=64)
             nc.vector.tensor_copy(
-                out=grouped_z1[:], in_=z1_tiles[c][:].rearrange("p b (t f) -> p b f t", t=PACK)
+                out=grouped_z1[:].rearrange("p b (c i) t -> p b c t i", i=RUN),
+                in_=z1_tiles[c][:].rearrange("p b (t c i) -> p b c t i", t=PACK, i=RUN),
             )
             return grouped_z1
 
@@ -131,24 +134,34 @@ def tile_manualchebconv_pb_t_kernel(tc, z0, z1, L_words, L_scales, out_0, out_1)
             quantise(grouped_z1, z1_codes, z1_scales)
             return z1_codes, z1_scales
 
-        z1_ready = [quantise_z1(regroup_z1(0)), quantise_z1(regroup_z1(1))]
-        z2_ready = []
-        for c in range(N_CHUNKS):
-            z2 = finish(copy_out(multiply(*z1_ready[c])), z0_tiles[c], out_0, c)
-            grouped_z2 = quant.tile([P, CHUNK, FEATS, PACK], BF16, align_bytes=64)
+        def regroup_z2(z2):
+            grouped_z2 = z2_quant.tile([P, CHUNK, FEATS, PACK], BF16, align_bytes=64)
             for b in range(CHUNK):
                 nc.scalar.copy(
-                    out=grouped_z2[:, b, :, :],
-                    in_=z2[:, b, :].rearrange("p (t f) -> p f t", t=PACK),
+                    out=grouped_z2[:, b, :, :].rearrange("p (c i) t -> p c t i", i=RUN),
+                    in_=z2[:, b, :].rearrange("p (t c i) -> p c t i", t=PACK, i=RUN),
                 )
-            if c + 2 < N_CHUNKS:
-                grouped_z1 = regroup_z1(c + 2)
+            return grouped_z2
+
+        def quantise_z2(grouped_z2, c):
             z2_codes = keep.tile([P, CHUNK * FEATS], U32, name="z2_codes_%d" % c, align_bytes=64)
             z2_scales = keep.tile([P, CHUNK * FEATS], U8, name="z2_scales_%d" % c, align_bytes=64)
             quantise(grouped_z2, z2_codes, z2_scales)
-            z2_ready.append((z2_codes, z2_scales))
+            return z2_codes, z2_scales
+
+        z1_ready = [quantise_z1(regroup_z1(0)), quantise_z1(regroup_z1(1))]
+        z2_grouped = []
+        z2_ready = []
+        for c in range(N_CHUNKS):
+            z2 = finish(copy_out(multiply(*z1_ready[c])), z0_tiles[c], out_0, c)
+            z2_grouped.append(regroup_z2(z2))
+            if c + 2 < N_CHUNKS:
+                grouped_z1 = regroup_z1(c + 2)
+            if c >= 1:
+                z2_ready.append(quantise_z2(z2_grouped[c - 1], c - 1))
             if c + 2 < N_CHUNKS:
                 z1_ready.append(quantise_z1(grouped_z1))
+        z2_ready.append(quantise_z2(z2_grouped[N_CHUNKS - 1], N_CHUNKS - 1))
 
         banks = multiply(*z2_ready[0])
         for c in range(N_CHUNKS):

@@ -19,6 +19,7 @@ NODES = P * PACK
 FEATS = 128
 CHUNK = 4
 N_CHUNKS = BATCH // CHUNK
+Z2_LATER = 2
 RUN = 4
 
 FLOPS = 2 * 2 * BATCH * NODES * NODES * FEATS
@@ -101,7 +102,7 @@ def tile_manualchebconv_pb_t_kernel(tc, z0, z1, L_words, L_scales, out_0, out_1)
                 sorted_rows.append(by_feature)
             return sorted_rows
 
-        def finish(sorted_rows, older, out, c):
+        def finish(sorted_rows, older_term, out, c, last):
             result = results.tile([P, CHUNK, NODES], F32)
             for b in range(CHUNK):
                 turned = turned_pool.tile([P, PACK, FEATS], F32)
@@ -113,11 +114,16 @@ def tile_manualchebconv_pb_t_kernel(tc, z0, z1, L_words, L_scales, out_0, out_1)
                     out=result[:, b, :],
                     in0=turned[:].rearrange("p t f -> p (t f)"),
                     scalar=2.0,
-                    in1=older[:, b, :],
+                    in1=older_term[:, b, :],
                     op0=MULT,
                     op1=SUBTRACT,
                 )
-            nc.sync.dma_start(out=by_partition(out, c), in_=result[:])
+                if last:
+                    nc.sync.dma_start(
+                        out=by_partition(out, c)[:, b : b + 1, :], in_=result[:, b : b + 1, :]
+                    )
+            if not last:
+                nc.sync.dma_start(out=by_partition(out, c), in_=result[:])
             return result
 
         def regroup_z1(c):
@@ -149,23 +155,28 @@ def tile_manualchebconv_pb_t_kernel(tc, z0, z1, L_words, L_scales, out_0, out_1)
             quantise(grouped_z2, z2_codes, z2_scales)
             return z2_codes, z2_scales
 
-        z1_ready = [quantise_z1(regroup_z1(0)), quantise_z1(regroup_z1(1))]
+        older = z0_tiles + z1_tiles
+        outs = [out_0] * N_CHUNKS + [out_1] * N_CHUNKS
+        n_rounds = 2 * N_CHUNKS
+        operands = [quantise_z1(regroup_z1(0)), quantise_z1(regroup_z1(1))]
+        z2_tiles = []
         z2_grouped = []
         z2_ready = []
-        for c in range(N_CHUNKS):
-            z2 = finish(copy_out(multiply(*z1_ready[c])), z0_tiles[c], out_0, c)
-            z2_grouped.append(regroup_z2(z2))
-            if c + 2 < N_CHUNKS:
-                grouped_z1 = regroup_z1(c + 2)
-            if c >= 1:
-                z2_ready.append(quantise_z2(z2_grouped[c - 1], c - 1))
-            if c + 2 < N_CHUNKS:
-                z1_ready.append(quantise_z1(grouped_z1))
-        z2_ready.append(quantise_z2(z2_grouped[N_CHUNKS - 1], N_CHUNKS - 1))
-
-        banks = multiply(*z2_ready[0])
-        for c in range(N_CHUNKS):
+        banks = multiply(*operands[0])
+        for r in range(n_rounds):
             sorted_rows = copy_out(banks)
-            if c + 1 < N_CHUNKS:
-                banks = multiply(*z2_ready[c + 1])
-            finish(sorted_rows, z1_tiles[c], out_1, c)
+            if r + 1 < n_rounds:
+                banks = multiply(*operands[r + 1])
+            result = finish(sorted_rows, older[r], outs[r], r % N_CHUNKS, last=(r == n_rounds - 1))
+            if r < N_CHUNKS:
+                z2_tiles.append(result)
+            if Z2_LATER <= r < N_CHUNKS + Z2_LATER:
+                z2_grouped.append(regroup_z2(z2_tiles[r - Z2_LATER]))
+            if r + 2 < N_CHUNKS:
+                grouped_z1 = regroup_z1(r + 2)
+            if Z2_LATER + 1 <= r < N_CHUNKS + Z2_LATER + 1:
+                z2_ready.append(quantise_z2(z2_grouped[r - Z2_LATER - 1], r - Z2_LATER - 1))
+            if r + 2 < N_CHUNKS:
+                operands.append(quantise_z1(grouped_z1))
+            elif r + 2 < n_rounds:
+                operands.append(z2_ready[r + 2 - N_CHUNKS])

@@ -19,7 +19,7 @@ NODES = P * PACK
 FEATS = 128
 CHUNK = 4
 N_CHUNKS = BATCH // CHUNK
-Z2_LATER = 2
+Z2_LATER = 1
 RUN = 4
 
 FLOPS = 2 * 2 * BATCH * NODES * NODES * FEATS
@@ -165,9 +165,12 @@ def tile_manualchebconv_pb_t_kernel(tc, z0, z1, L_words, L_scales, out_0, out_1)
         banks = multiply(*operands[0])
         for r in range(n_rounds):
             sorted_rows = copy_out(banks)
-            if r + 1 < n_rounds:
+            multiply_first = N_CHUNKS <= r + 1 < n_rounds
+            if multiply_first:
                 banks = multiply(*operands[r + 1])
             result = finish(sorted_rows, older[r], outs[r], r % N_CHUNKS, last=(r == n_rounds - 1))
+            if r + 1 < N_CHUNKS:
+                banks = multiply(*operands[r + 1])
             if r < N_CHUNKS:
                 z2_tiles.append(result)
             if Z2_LATER <= r < N_CHUNKS + Z2_LATER:

@@ -11,6 +11,7 @@ U8 = mybir.dt.uint8
 FP8X4 = mybir.dt.float8_e4m3fn_x4
 MULT = mybir.AluOpType.mult
 SUBTRACT = mybir.AluOpType.subtract
+ADD = mybir.AluOpType.add
 
 P = 128
 PACK = 4
@@ -20,6 +21,7 @@ FEATS = 128
 CHUNK = 4
 N_CHUNKS = BATCH // CHUNK
 Z2_LATER = 1
+VECTOR_CHUNKS = 2
 RUN = 4
 
 FLOPS = 2 * 2 * BATCH * NODES * NODES * FEATS
@@ -33,7 +35,7 @@ def tile_manualchebconv_pb_t_kernel(tc, z0, z1, L_words, L_scales, out_0, out_1)
     nc = tc.nc
     with ExitStack() as stack:
         keep = stack.enter_context(tc.tile_pool(name="keep", bufs=1))
-        z1_quant = stack.enter_context(tc.tile_pool(name="z1_quant", bufs=2))
+        z1_quant = stack.enter_context(tc.tile_pool(name="z1_quant", bufs=4))
         z2_quant = stack.enter_context(tc.tile_pool(name="z2_quant", bufs=3))
         z1_mx = stack.enter_context(tc.tile_pool(name="z1_mx", bufs=3))
         rows = stack.enter_context(tc.tile_pool(name="rows", bufs=2 * CHUNK))
@@ -128,10 +130,21 @@ def tile_manualchebconv_pb_t_kernel(tc, z0, z1, L_words, L_scales, out_0, out_1)
 
         def regroup_z1(c):
             grouped_z1 = z1_quant.tile([P, CHUNK, FEATS, PACK], BF16, align_bytes=64)
-            nc.vector.tensor_copy(
-                out=grouped_z1[:].rearrange("p b (c i) t -> p b c t i", i=RUN),
-                in_=z1_tiles[c][:].rearrange("p b (t c i) -> p b c t i", t=PACK, i=RUN),
-            )
+            if c < VECTOR_CHUNKS:
+                nc.vector.tensor_copy(
+                    out=grouped_z1[:].rearrange("p b (c i) t -> p b c t i", i=RUN),
+                    in_=z1_tiles[c][:].rearrange("p b (t c i) -> p b c t i", t=PACK, i=RUN),
+                )
+            else:
+                for b in range(CHUNK):
+                    nc.gpsimd.tensor_scalar(
+                        out=grouped_z1[:, b, :, :],
+                        in0=z1_tiles[c][:, b, :].rearrange("p (t f) -> p f t", t=PACK),
+                        scalar1=1.0,
+                        scalar2=0.0,
+                        op0=MULT,
+                        op1=ADD,
+                    )
             return grouped_z1
 
         def quantise_z1(grouped_z1):

@@ -22,6 +22,7 @@ CHUNK = 4
 N_CHUNKS = BATCH // CHUNK
 Z2_LATER = 1
 VECTOR_CHUNKS = 2
+VECTOR_BANKS = 1
 RUN = 4
 
 FLOPS = 2 * 2 * BATCH * NODES * NODES * FEATS
@@ -94,13 +95,15 @@ def tile_manualchebconv_pb_t_kernel(tc, z0, z1, L_words, L_scales, out_0, out_1)
                 banks.append(sums)
             return banks
 
-        def copy_out(banks):
+        def copy_out(banks, vector_banks):
             sorted_rows = []
-            for sums in banks:
+            for b in range(CHUNK):
                 by_feature = rows.tile([P, PACK, P], F32)
-                nc.scalar.copy(
-                    out=by_feature[:], in_=sums[:].rearrange("f (p t) -> f t p", t=PACK)
-                )
+                sorted_view = banks[b][:].rearrange("f (p t) -> f t p", t=PACK)
+                if b < CHUNK - vector_banks:
+                    nc.scalar.copy(out=by_feature[:], in_=sorted_view)
+                else:
+                    nc.vector.tensor_copy(out=by_feature[:], in_=sorted_view)
                 sorted_rows.append(by_feature)
             return sorted_rows
 
@@ -177,7 +180,8 @@ def tile_manualchebconv_pb_t_kernel(tc, z0, z1, L_words, L_scales, out_0, out_1)
         z2_ready = []
         banks = multiply(*operands[0])
         for r in range(n_rounds):
-            sorted_rows = copy_out(banks)
+            scalar_regroups = Z2_LATER <= r < N_CHUNKS + Z2_LATER
+            sorted_rows = copy_out(banks, VECTOR_BANKS if scalar_regroups else 0)
             multiply_first = N_CHUNKS <= r + 1 < n_rounds
             if multiply_first:
                 banks = multiply(*operands[r + 1])
@@ -186,7 +190,7 @@ def tile_manualchebconv_pb_t_kernel(tc, z0, z1, L_words, L_scales, out_0, out_1)
                 banks = multiply(*operands[r + 1])
             if r < N_CHUNKS:
                 z2_tiles.append(result)
-            if Z2_LATER <= r < N_CHUNKS + Z2_LATER:
+            if scalar_regroups:
                 z2_grouped.append(regroup_z2(z2_tiles[r - Z2_LATER]))
             if r + 2 < N_CHUNKS:
                 grouped_z1 = regroup_z1(r + 2)

@@ -1,7 +1,6 @@
 from contextlib import ExitStack
 
 import concourse.mybir as mybir
-from concourse.masks import make_identity
 
 F32 = mybir.dt.float32
 BF16 = mybir.dt.bfloat16
@@ -11,7 +10,6 @@ U8 = mybir.dt.uint8
 FP8X4 = mybir.dt.float8_e4m3fn_x4
 MULT = mybir.AluOpType.mult
 SUBTRACT = mybir.AluOpType.subtract
-ADD = mybir.AluOpType.add
 
 P = 128
 PACK = 4
@@ -20,9 +18,6 @@ NODES = P * PACK
 FEATS = 128
 CHUNK = 4
 N_CHUNKS = BATCH // CHUNK
-Z2_LATER = 1
-VECTOR_CHUNKS = 2
-VECTOR_BANKS = 1
 RUN = 4
 
 FLOPS = 2 * 2 * BATCH * NODES * NODES * FEATS
@@ -36,21 +31,16 @@ def tile_manualchebconv_pb_t_kernel(tc, z0, z1, L_words, L_scales, out_0, out_1)
     nc = tc.nc
     with ExitStack() as stack:
         keep = stack.enter_context(tc.tile_pool(name="keep", bufs=1))
-        z1_quant = stack.enter_context(tc.tile_pool(name="z1_quant", bufs=4))
-        z2_quant = stack.enter_context(tc.tile_pool(name="z2_quant", bufs=3))
-        z1_mx = stack.enter_context(tc.tile_pool(name="z1_mx", bufs=3))
-        rows = stack.enter_context(tc.tile_pool(name="rows", bufs=2 * CHUNK))
-        results = stack.enter_context(tc.tile_pool(name="results", bufs=7))
-        sums_pool = stack.enter_context(tc.psum_pool(name="sums", bufs=CHUNK))
-        turned_pool = stack.enter_context(tc.psum_pool(name="turned", bufs=CHUNK))
+        grouped_pool = stack.enter_context(tc.tile_pool(name="grouped", bufs=3))
+        mx_pool = stack.enter_context(tc.tile_pool(name="mx", bufs=3))
+        results = stack.enter_context(tc.tile_pool(name="results", bufs=10))
+        sums1_pool = stack.enter_context(tc.psum_pool(name="sums1", bufs=CHUNK))
+        sums2_pool = stack.enter_context(tc.psum_pool(name="sums2", bufs=CHUNK))
         stack.enter_context(tc.manual_schedule())
 
-        identity = keep.tile([P, P], F32)
-        make_identity(nc, identity[:])
-
-        w_words = keep.tile([P, NODES * PACK], U8, align_bytes=64)
-        w_scales = keep.tile([P, NODES], U8, align_bytes=64)
-        nc.vector.memset(w_scales[:].bitcast(I32), 0)
+        w_raw = keep.tile([P, NODES], I32)
+        ws_raw = keep.tile([P, NODES], U8)
+        nc.vector.memset(ws_raw[:].bitcast(I32), 0)
 
         z0_tiles = [keep.tile([P, CHUNK, NODES], BF16, name="z0_%d" % c) for c in range(N_CHUNKS)]
         z1_tiles = [keep.tile([P, CHUNK, NODES], BF16, name="z1_%d" % c) for c in range(N_CHUNKS)]
@@ -59,144 +49,108 @@ def tile_manualchebconv_pb_t_kernel(tc, z0, z1, L_words, L_scales, out_0, out_1)
         scale_rows = L_scales.rearrange("g q n -> (g q) n")
         for quadrant in range(4):
             nc.sync.dma_start(
-                out=w_scales[32 * quadrant : 32 * quadrant + 4, :].bitcast(I32),
+                out=ws_raw[32 * quadrant : 32 * quadrant + 4, :].bitcast(I32),
                 in_=scale_rows[4 * quadrant : 4 * quadrant + 4, :].bitcast(I32),
             )
         nc.sync.dma_start(
-            out=w_words[:].bitcast(I32),
-            in_=L_words.rearrange("g p n t -> (g p) (n t)").bitcast(I32),
+            out=w_raw[:], in_=L_words.rearrange("g p n t -> (g p) (n t)").bitcast(I32)
         )
         for c in range(N_CHUNKS):
             if c + 1 < N_CHUNKS:
                 nc.sync.dma_start(out=z1_tiles[c + 1][:], in_=by_partition(z1, c + 1))
             nc.sync.dma_start(out=z0_tiles[c][:], in_=by_partition(z0, c))
 
-        def quantise(grouped, codes, scales):
+        def regroup(engine_copy, grouped, source, b):
+            engine_copy(
+                out=grouped[:, b, :, :].rearrange("p (c i) t -> p c t i", i=RUN),
+                in_=source[:, b, :].rearrange("p (t c i) -> p c t i", t=PACK, i=RUN),
+            )
+
+        def quantise(grouped):
+            codes = mx_pool.tile([P, CHUNK * FEATS], U32, align_bytes=64)
+            scales = mx_pool.tile([P, CHUNK * FEATS], U8, align_bytes=64)
             nc.vector.quantize_mx(
                 out=codes[:].bitcast(FP8X4),
                 scales=scales[:],
                 in_=grouped[:].rearrange("p b f t -> p (b f t)"),
             )
+            return codes, scales
 
-        def multiply(codes, scales):
+        def multiply(pool, operand):
+            codes, scales = operand
             banks = []
             for b in range(CHUNK):
-                sums = sums_pool.tile([P, NODES], F32)
+                sums = pool.tile([P, PACK, FEATS], F32)
                 cols = slice(b * FEATS, (b + 1) * FEATS)
-                nc.tensor.matmul_mx(
-                    out=sums[:],
-                    lhsT=codes[:, cols].bitcast(FP8X4),
-                    lhsT_scale=scales[:, cols],
-                    rhs=w_words[:].bitcast(FP8X4),
-                    rhs_scale=w_scales[:],
-                    start=True,
-                    stop=True,
-                )
+                for j in range(PACK):
+                    nc.tensor.matmul_mx(
+                        out=sums[:, j, :],
+                        lhsT=w_sorted[:, j, :].bitcast(FP8X4),
+                        lhsT_scale=ws_sorted[:, j, :],
+                        rhs=codes[:, cols].bitcast(FP8X4),
+                        rhs_scale=scales[:, cols],
+                        start=True,
+                        stop=True,
+                    )
                 banks.append(sums)
             return banks
 
-        def copy_out(banks, vector_banks):
-            sorted_rows = []
+        def combine(result, banks, older_term, b):
+            nc.vector.scalar_tensor_tensor(
+                out=result[:, b, :],
+                in0=banks[b][:].rearrange("p j f -> p (j f)"),
+                scalar=2.0,
+                in1=older_term[:, b, :],
+                op0=MULT,
+                op1=SUBTRACT,
+            )
+
+        z1_grouped = {}
+        z2_grouped = {}
+        step1 = {}
+        step2 = {}
+        for c in range(2):
+            grouped_z1 = grouped_pool.tile([P, CHUNK, FEATS, PACK], BF16, align_bytes=64)
             for b in range(CHUNK):
-                by_feature = rows.tile([P, PACK, P], F32)
-                sorted_view = banks[b][:].rearrange("f (p t) -> f t p", t=PACK)
-                if b < CHUNK - vector_banks:
-                    nc.scalar.copy(out=by_feature[:], in_=sorted_view)
-                else:
-                    nc.vector.tensor_copy(out=by_feature[:], in_=sorted_view)
-                sorted_rows.append(by_feature)
-            return sorted_rows
+                regroup(nc.vector.tensor_copy if c == 0 else nc.scalar.copy, grouped_z1, z1_tiles[c], b)
+            z1_grouped[c] = grouped_z1
+        w_sorted = keep.tile([P, PACK, P], I32, align_bytes=64)
+        ws_sorted = keep.tile([P, PACK, P], U8, align_bytes=64)
+        nc.vector.tensor_copy(
+            out=ws_sorted[:].rearrange("p j m -> p m j"),
+            in_=ws_raw[:].rearrange("p (m j) -> p m j", j=PACK),
+        )
+        nc.vector.tensor_copy(
+            out=w_sorted[:], in_=w_raw[:].rearrange("p (m j) -> p j m", j=PACK)
+        )
+        step1[0] = multiply(sums1_pool, quantise(z1_grouped[0]))
 
-        def finish(sorted_rows, older_term, out, c, last):
-            result = results.tile([P, CHUNK, NODES], F32)
-            for b in range(CHUNK):
-                turned = turned_pool.tile([P, PACK, FEATS], F32)
-                for t in range(PACK):
-                    nc.tensor.transpose(
-                        out=turned[:, t, :], in_=sorted_rows[b][:, t, :], identity=identity[:]
-                    )
-                nc.vector.scalar_tensor_tensor(
-                    out=result[:, b, :],
-                    in0=turned[:].rearrange("p t f -> p (t f)"),
-                    scalar=2.0,
-                    in1=older_term[:, b, :],
-                    op0=MULT,
-                    op1=SUBTRACT,
-                )
-                if last:
-                    nc.sync.dma_start(
-                        out=by_partition(out, c)[:, b : b + 1, :], in_=result[:, b : b + 1, :]
-                    )
-            if not last:
-                nc.sync.dma_start(out=by_partition(out, c), in_=result[:])
-            return result
-
-        def regroup_z1(c):
-            grouped_z1 = z1_quant.tile([P, CHUNK, FEATS, PACK], BF16, align_bytes=64)
-            if c < VECTOR_CHUNKS:
-                nc.vector.tensor_copy(
-                    out=grouped_z1[:].rearrange("p b (c i) t -> p b c t i", i=RUN),
-                    in_=z1_tiles[c][:].rearrange("p b (t c i) -> p b c t i", t=PACK, i=RUN),
-                )
-            else:
-                for b in range(CHUNK):
-                    nc.gpsimd.tensor_scalar(
-                        out=grouped_z1[:, b, :, :],
-                        in0=z1_tiles[c][:, b, :].rearrange("p (t f) -> p f t", t=PACK),
-                        scalar1=1.0,
-                        scalar2=0.0,
-                        op0=MULT,
-                        op1=ADD,
-                    )
-            return grouped_z1
-
-        def quantise_z1(grouped_z1):
-            z1_codes = z1_mx.tile([P, CHUNK * FEATS], U32, align_bytes=64)
-            z1_scales = z1_mx.tile([P, CHUNK * FEATS], U8, align_bytes=64)
-            quantise(grouped_z1, z1_codes, z1_scales)
-            return z1_codes, z1_scales
-
-        def regroup_z2(z2):
-            grouped_z2 = z2_quant.tile([P, CHUNK, FEATS, PACK], BF16, align_bytes=64)
-            for b in range(CHUNK):
-                nc.scalar.copy(
-                    out=grouped_z2[:, b, :, :].rearrange("p (c i) t -> p c t i", i=RUN),
-                    in_=z2[:, b, :].rearrange("p (t c i) -> p c t i", t=PACK, i=RUN),
-                )
-            return grouped_z2
-
-        def quantise_z2(grouped_z2, c):
-            z2_codes = keep.tile([P, CHUNK * FEATS], U32, name="z2_codes_%d" % c, align_bytes=64)
-            z2_scales = keep.tile([P, CHUNK * FEATS], U8, name="z2_scales_%d" % c, align_bytes=64)
-            quantise(grouped_z2, z2_codes, z2_scales)
-            return z2_codes, z2_scales
-
-        older = z0_tiles + z1_tiles
-        outs = [out_0] * N_CHUNKS + [out_1] * N_CHUNKS
-        n_rounds = 2 * N_CHUNKS
-        operands = [quantise_z1(regroup_z1(0)), quantise_z1(regroup_z1(1))]
-        z2_tiles = []
-        z2_grouped = []
-        z2_ready = []
-        banks = multiply(*operands[0])
-        for r in range(n_rounds):
-            scalar_regroups = Z2_LATER <= r < N_CHUNKS + Z2_LATER
-            sorted_rows = copy_out(banks, VECTOR_BANKS if scalar_regroups else 0)
-            multiply_first = N_CHUNKS <= r + 1 < n_rounds
-            if multiply_first:
-                banks = multiply(*operands[r + 1])
-            result = finish(sorted_rows, older[r], outs[r], r % N_CHUNKS, last=(r == n_rounds - 1))
-            if r + 1 < N_CHUNKS:
-                banks = multiply(*operands[r + 1])
+        for r in range(N_CHUNKS + 1):
+            if r >= 1:
+                step2[r - 1] = multiply(sums2_pool, quantise(z2_grouped[r - 1]))
             if r < N_CHUNKS:
-                z2_tiles.append(result)
-            if scalar_regroups:
-                z2_grouped.append(regroup_z2(z2_tiles[r - Z2_LATER]))
+                z2 = results.tile([P, CHUNK, NODES], F32, name="result")
+                grouped_z2 = grouped_pool.tile([P, CHUNK, FEATS, PACK], BF16, align_bytes=64)
+                for b in range(CHUNK):
+                    combine(z2, step1[r], z0_tiles[r], b)
+                    regroup(nc.scalar.copy, grouped_z2, z2, b)
+                z2_grouped[r] = grouped_z2
+                nc.sync.dma_start(out=by_partition(out_0, r), in_=z2[:])
+            if r + 1 < N_CHUNKS:
+                step1[r + 1] = multiply(sums1_pool, quantise(z1_grouped[r + 1]))
             if r + 2 < N_CHUNKS:
-                grouped_z1 = regroup_z1(r + 2)
-            if Z2_LATER + 1 <= r < N_CHUNKS + Z2_LATER + 1:
-                z2_ready.append(quantise_z2(z2_grouped[r - Z2_LATER - 1], r - Z2_LATER - 1))
-            if r + 2 < N_CHUNKS:
-                operands.append(quantise_z1(grouped_z1))
-            elif r + 2 < n_rounds:
-                operands.append(z2_ready[r + 2 - N_CHUNKS])
+                grouped_z1 = grouped_pool.tile([P, CHUNK, FEATS, PACK], BF16, align_bytes=64)
+                for b in range(CHUNK):
+                    regroup(nc.scalar.copy, grouped_z1, z1_tiles[r + 2], b)
+                z1_grouped[r + 2] = grouped_z1
+            if r >= 1:
+                z3 = results.tile([P, CHUNK, NODES], F32, name="result")
+                last = r == N_CHUNKS
+                for b in range(CHUNK):
+                    combine(z3, step2[r - 1], z1_tiles[r - 1], b)
+                    if last:
+                        nc.sync.dma_start(
+                            out=by_partition(out_1, r - 1)[:, b : b + 1, :], in_=z3[:, b : b + 1, :]
+                        )
+                if not last:
+                    nc.sync.dma_start(out=by_partition(out_1, r - 1), in_=z3[:])

@@ -149,8 +149,8 @@ def tile_manualchebconv_pb_t_kernel(tc, z0, z1, L_words, L_scales, out_0, out_1)
                 for b in range(CHUNK):
                     combine(z3, step2[r - 1], z1_tiles[r - 1], b)
                     if last:
-                        nc.sync.dma_start(
+                        (nc.scalar if b % 2 == 0 else nc.sync).dma_start(
                             out=by_partition(out_1, r - 1)[:, b : b + 1, :], in_=z3[:, b : b + 1, :]
                         )
                 if not last:
-                    nc.sync.dma_start(out=by_partition(out_1, r - 1), in_=z3[:])
+                    nc.scalar.dma_start(out=by_partition(out_1, r - 1), in_=z3[:])

@@ -18,6 +18,7 @@ NODES = P * PACK
 FEATS = 128
 CHUNK = 4
 N_CHUNKS = BATCH // CHUNK
+DMA_ALIGN = 256
 RUN = 4
 
 FLOPS = 2 * 2 * BATCH * NODES * NODES * FEATS
@@ -38,12 +39,18 @@ def tile_manualchebconv_pb_t_kernel(tc, z0, z1, L_words, L_scales, out_0, out_1)
         sums2_pool = stack.enter_context(tc.psum_pool(name="sums2", bufs=CHUNK))
         stack.enter_context(tc.manual_schedule())
 
-        w_raw = keep.tile([P, NODES], I32)
+        w_raw = keep.tile([P, NODES], I32, align_bytes=DMA_ALIGN)
         ws_raw = keep.tile([P, NODES], U8)
         nc.vector.memset(ws_raw[:].bitcast(I32), 0)
 
-        z0_tiles = [keep.tile([P, CHUNK, NODES], BF16, name="z0_%d" % c) for c in range(N_CHUNKS)]
-        z1_tiles = [keep.tile([P, CHUNK, NODES], BF16, name="z1_%d" % c) for c in range(N_CHUNKS)]
+        z0_tiles = [
+            keep.tile([P, CHUNK, NODES], BF16, name="z0_%d" % c, align_bytes=DMA_ALIGN)
+            for c in range(N_CHUNKS)
+        ]
+        z1_tiles = [
+            keep.tile([P, CHUNK, NODES], BF16, name="z1_%d" % c, align_bytes=DMA_ALIGN)
+            for c in range(N_CHUNKS)
+        ]
 
         nc.sync.dma_start(out=z1_tiles[0][:], in_=by_partition(z1, 0))
         scale_rows = L_scales.rearrange("g q n -> (g q) n")
@@ -129,7 +136,7 @@ def tile_manualchebconv_pb_t_kernel(tc, z0, z1, L_words, L_scales, out_0, out_1)
             if r >= 1:
                 step2[r - 1] = multiply(sums2_pool, quantise(z2_grouped[r - 1]))
             if r < N_CHUNKS:
-                z2 = results.tile([P, CHUNK, NODES], F32, name="result")
+                z2 = results.tile([P, CHUNK, NODES], F32, name="result", align_bytes=DMA_ALIGN)
                 grouped_z2 = grouped_pool.tile([P, CHUNK, FEATS, PACK], BF16, align_bytes=64)
                 for b in range(CHUNK):
                     combine(z2, step1[r], z0_tiles[r], b)
@@ -144,7 +151,7 @@ def tile_manualchebconv_pb_t_kernel(tc, z0, z1, L_words, L_scales, out_0, out_1)
                     regroup(nc.scalar.copy, grouped_z1, z1_tiles[r + 2], b)
                 z1_grouped[r + 2] = grouped_z1
             if r >= 1:
-                z3 = results.tile([P, CHUNK, NODES], F32, name="result")
+                z3 = results.tile([P, CHUNK, NODES], F32, name="result", align_bytes=DMA_ALIGN)
                 last = r == N_CHUNKS
                 for b in range(CHUNK):
                     combine(z3, step2[r - 1], z1_tiles[r - 1], b)

@@ -18,7 +18,7 @@ NODES = P * PACK
 FEATS = 128
 CHUNK = 4
 N_CHUNKS = BATCH // CHUNK
-DMA_ALIGN = 256
+DMA_ALIGN = 2048
 RUN = 4
 
 FLOPS = 2 * 2 * BATCH * NODES * NODES * FEATS

@@ -83,15 +83,17 @@ def tile_manualchebconv_pb_t_kernel(tc, z0, z1, L_words, L_scales, out_0, out_1)
             )
             return codes, scales
 
-        def multiply(pool, operand):
+        def multiply(pool, operand, by_items):
             codes, scales = operand
             banks = []
-            for b in range(CHUNK):
-                sums = pool.tile([P, PACK, FEATS], F32)
-                cols = slice(b * FEATS, (b + 1) * FEATS)
-                for j in range(PACK):
+            for i in range(CHUNK):
+                sums = pool.tile([P, PACK * FEATS], F32)
+                for k in range(PACK if by_items else 1):
+                    j = k if by_items else i
+                    cols = slice(i * FEATS, (i + 1) * FEATS) if by_items else slice(0, CHUNK * FEATS)
+                    outs = slice(k * FEATS, (k + 1) * FEATS) if by_items else slice(0, CHUNK * FEATS)
                     nc.tensor.matmul_mx(
-                        out=sums[:, j, :],
+                        out=sums[:, outs],
                         lhsT=w_sorted[:, j, :].bitcast(FP8X4),
                         lhsT_scale=ws_sorted[:, j, :],
                         rhs=codes[:, cols].bitcast(FP8X4),
@@ -102,12 +104,18 @@ def tile_manualchebconv_pb_t_kernel(tc, z0, z1, L_words, L_scales, out_0, out_1)
                 banks.append(sums)
             return banks
 
-        def combine(result, banks, older_term, b):
+        def combine(result, banks, older_term, i, by_items):
+            if by_items:
+                part = lambda t: t[:, i, :]
+                product = banks[i][:]
+            else:
+                part = lambda t: t[:, :, i * FEATS : (i + 1) * FEATS]
+                product = banks[i][:].rearrange("p (b f) -> p b f", b=CHUNK)
             nc.vector.scalar_tensor_tensor(
-                out=result[:, b, :],
-                in0=banks[b][:].rearrange("p j f -> p (j f)"),
+                out=part(result),
+                in0=product,
                 scalar=2.0,
-                in1=older_term[:, b, :],
+                in1=part(older_term),
                 op0=MULT,
                 op1=SUBTRACT,
             )
@@ -130,34 +138,45 @@ def tile_manualchebconv_pb_t_kernel(tc, z0, z1, L_words, L_scales, out_0, out_1)
         nc.vector.tensor_copy(
             out=w_sorted[:], in_=w_raw[:].rearrange("p (m j) -> p j m", j=PACK)
         )
-        step1[0] = multiply(sums1_pool, quantise(z1_grouped[0]))
+        by_items = [c == 0 or c == N_CHUNKS - 1 for c in range(N_CHUNKS)]
+        step1[0] = multiply(sums1_pool, quantise(z1_grouped[0]), by_items[0])
+
+        def regroup_z1(c):
+            grouped_z1 = grouped_pool.tile([P, CHUNK, FEATS, PACK], BF16, align_bytes=64)
+            for b in range(CHUNK):
+                regroup(nc.scalar.copy, grouped_z1, z1_tiles[c], b)
+            z1_grouped[c] = grouped_z1
 
         for r in range(N_CHUNKS + 1):
             if r >= 1:
-                step2[r - 1] = multiply(sums2_pool, quantise(z2_grouped[r - 1]))
+                step2[r - 1] = multiply(
+                    sums2_pool, quantise(z2_grouped[r - 1]), by_items[r - 1]
+                )
             if r < N_CHUNKS:
+                if r + 2 < N_CHUNKS and not by_items[r]:
+                    regroup_z1(r + 2)
                 z2 = results.tile([P, CHUNK, NODES], F32, name="result", align_bytes=DMA_ALIGN)
                 grouped_z2 = grouped_pool.tile([P, CHUNK, FEATS, PACK], BF16, align_bytes=64)
+                for i in range(CHUNK):
+                    combine(z2, step1[r], z0_tiles[r], i, by_items[r])
                 for b in range(CHUNK):
-                    combine(z2, step1[r], z0_tiles[r], b)
                     regroup(nc.scalar.copy, grouped_z2, z2, b)
                 z2_grouped[r] = grouped_z2
                 nc.sync.dma_start(out=by_partition(out_0, r), in_=z2[:])
             if r + 1 < N_CHUNKS:
-                step1[r + 1] = multiply(sums1_pool, quantise(z1_grouped[r + 1]))
-            if r + 2 < N_CHUNKS:
-                grouped_z1 = grouped_pool.tile([P, CHUNK, FEATS, PACK], BF16, align_bytes=64)
-                for b in range(CHUNK):
-                    regroup(nc.scalar.copy, grouped_z1, z1_tiles[r + 2], b)
-                z1_grouped[r + 2] = grouped_z1
+                step1[r + 1] = multiply(
+                    sums1_pool, quantise(z1_grouped[r + 1]), by_items[r + 1]
+                )
+            if r + 2 < N_CHUNKS and by_items[r]:
+                regroup_z1(r + 2)
             if r >= 1:
                 z3 = results.tile([P, CHUNK, NODES], F32, name="result", align_bytes=DMA_ALIGN)
                 last = r == N_CHUNKS
-                for b in range(CHUNK):
-                    combine(z3, step2[r - 1], z1_tiles[r - 1], b)
+                for i in range(CHUNK):
+                    combine(z3, step2[r - 1], z1_tiles[r - 1], i, by_items[r - 1])
                     if last:
-                        (nc.scalar if b % 2 == 0 else nc.sync).dma_start(
-                            out=by_partition(out_1, r - 1)[:, b : b + 1, :], in_=z3[:, b : b + 1, :]
+                        (nc.scalar if i % 2 == 0 else nc.sync).dma_start(
+                            out=by_partition(out_1, r - 1)[:, i : i + 1, :], in_=z3[:, i : i + 1, :]
                         )
                 if not last:
                     nc.scalar.dma_start(out=by_partition(out_1, r - 1), in_=z3[:])

@@ -52,7 +52,10 @@ def tile_manualchebconv_pb_t_kernel(tc, z0, z1, L_words, L_scales, out_0, out_1)
             for c in range(N_CHUNKS)
         ]
 
-        nc.sync.dma_start(out=z1_tiles[0][:], in_=by_partition(z1, 0))
+        def load(tiles, dram, c):
+            nc.sync.dma_start(out=tiles[c][:].bitcast(F32), in_=by_partition(dram, c).bitcast(F32))
+
+        load(z1_tiles, z1, 0)
         scale_rows = L_scales.rearrange("g q n -> (g q) n")
         for quadrant in range(4):
             nc.sync.dma_start(
@@ -64,8 +67,8 @@ def tile_manualchebconv_pb_t_kernel(tc, z0, z1, L_words, L_scales, out_0, out_1)
         )
         for c in range(N_CHUNKS):
             if c + 1 < N_CHUNKS:
-                nc.sync.dma_start(out=z1_tiles[c + 1][:], in_=by_partition(z1, c + 1))
-            nc.sync.dma_start(out=z0_tiles[c][:], in_=by_partition(z0, c))
+                load(z1_tiles, z1, c + 1)
+            load(z0_tiles, z0, c)
 
         def regroup(engine_copy, grouped, source, b):
             engine_copy(

from contextlib import ExitStack

import concourse.mybir as mybir

F32 = mybir.dt.float32
BF16 = mybir.dt.bfloat16
I32 = mybir.dt.int32
U32 = mybir.dt.uint32
U8 = mybir.dt.uint8
FP8X4 = mybir.dt.float8_e4m3fn_x4
MULT = mybir.AluOpType.mult
SUBTRACT = mybir.AluOpType.subtract

P = 128
PACK = 4
BATCH = 32
NODES = P * PACK
FEATS = 128
CHUNK = 4
N_CHUNKS = BATCH // CHUNK
DMA_ALIGN = 2048
RUN = 4

FLOPS = 2 * 2 * BATCH * NODES * NODES * FEATS


def by_partition(dram, c):
    return dram[c * CHUNK : (c + 1) * CHUNK].rearrange("b (p t) f -> p b (t f)", t=PACK)


def tile_manualchebconv_pb_t_kernel(tc, z0, z1, L_words, L_scales, out_0, out_1):
    nc = tc.nc
    with ExitStack() as stack:
        keep = stack.enter_context(tc.tile_pool(name="keep", bufs=1))
        grouped_pool = stack.enter_context(tc.tile_pool(name="grouped", bufs=3))
        mx_pool = stack.enter_context(tc.tile_pool(name="mx", bufs=3))
        results = stack.enter_context(tc.tile_pool(name="results", bufs=10))
        sums1_pool = stack.enter_context(tc.psum_pool(name="sums1", bufs=CHUNK))
        sums2_pool = stack.enter_context(tc.psum_pool(name="sums2", bufs=CHUNK))
        stack.enter_context(tc.manual_schedule())

        w_raw = keep.tile([P, NODES], I32, align_bytes=DMA_ALIGN)
        ws_raw = keep.tile([P, NODES], U8)
        nc.vector.memset(ws_raw[:].bitcast(I32), 0)

        z0_tiles = [
            keep.tile([P, CHUNK, NODES], BF16, name="z0_%d" % c, align_bytes=DMA_ALIGN)
            for c in range(N_CHUNKS)
        ]
        z1_tiles = [
            keep.tile([P, CHUNK, NODES], BF16, name="z1_%d" % c, align_bytes=DMA_ALIGN)
            for c in range(N_CHUNKS)
        ]

        def load(tiles, dram, c):
            nc.sync.dma_start(out=tiles[c][:].bitcast(F32), in_=by_partition(dram, c).bitcast(F32))

        load(z1_tiles, z1, 0)
        scale_rows = L_scales.rearrange("g q n -> (g q) n")
        for quadrant in range(4):
            nc.sync.dma_start(
                out=ws_raw[32 * quadrant : 32 * quadrant + 4, :].bitcast(I32),
                in_=scale_rows[4 * quadrant : 4 * quadrant + 4, :].bitcast(I32),
            )
        nc.sync.dma_start(
            out=w_raw[:], in_=L_words.rearrange("g p n t -> (g p) (n t)").bitcast(I32)
        )
        for c in range(N_CHUNKS):
            if c + 1 < N_CHUNKS:
                load(z1_tiles, z1, c + 1)
            load(z0_tiles, z0, c)

        def regroup(engine_copy, grouped, source, b):
            engine_copy(
                out=grouped[:, b, :, :].rearrange("p (c i) t -> p c t i", i=RUN),
                in_=source[:, b, :].rearrange("p (t c i) -> p c t i", t=PACK, i=RUN),
            )

        def quantise(grouped):
            codes = mx_pool.tile([P, CHUNK * FEATS], U32, align_bytes=64)
            scales = mx_pool.tile([P, CHUNK * FEATS], U8, align_bytes=64)
            nc.vector.quantize_mx(
                out=codes[:].bitcast(FP8X4),
                scales=scales[:],
                in_=grouped[:].rearrange("p b f t -> p (b f t)"),
            )
            return codes, scales

        def multiply(pool, operand, by_items):
            codes, scales = operand
            banks = []
            for i in range(CHUNK):
                sums = pool.tile([P, PACK * FEATS], F32)
                for k in range(PACK if by_items else 1):
                    j = k if by_items else i
                    cols = slice(i * FEATS, (i + 1) * FEATS) if by_items else slice(0, CHUNK * FEATS)
                    outs = slice(k * FEATS, (k + 1) * FEATS) if by_items else slice(0, CHUNK * FEATS)
                    nc.tensor.matmul_mx(
                        out=sums[:, outs],
                        lhsT=w_sorted[:, j, :].bitcast(FP8X4),
                        lhsT_scale=ws_sorted[:, j, :],
                        rhs=codes[:, cols].bitcast(FP8X4),
                        rhs_scale=scales[:, cols],
                        start=True,
                        stop=True,
                    )
                banks.append(sums)
            return banks

        def combine(result, banks, older_term, i, by_items):
            if by_items:
                part = lambda t: t[:, i, :]
                product = banks[i][:]
            else:
                part = lambda t: t[:, :, i * FEATS : (i + 1) * FEATS]
                product = banks[i][:].rearrange("p (b f) -> p b f", b=CHUNK)
            nc.vector.scalar_tensor_tensor(
                out=part(result),
                in0=product,
                scalar=2.0,
                in1=part(older_term),
                op0=MULT,
                op1=SUBTRACT,
            )

        z1_grouped = {}
        z2_grouped = {}
        step1 = {}
        step2 = {}
        for c in range(2):
            grouped_z1 = grouped_pool.tile([P, CHUNK, FEATS, PACK], BF16, align_bytes=64)
            for b in range(CHUNK):
                regroup(nc.vector.tensor_copy if c == 0 else nc.scalar.copy, grouped_z1, z1_tiles[c], b)
            z1_grouped[c] = grouped_z1
        w_sorted = keep.tile([P, PACK, P], I32, align_bytes=64)
        ws_sorted = keep.tile([P, PACK, P], U8, align_bytes=64)
        nc.vector.tensor_copy(
            out=ws_sorted[:].rearrange("p j m -> p m j"),
            in_=ws_raw[:].rearrange("p (m j) -> p m j", j=PACK),
        )
        nc.vector.tensor_copy(
            out=w_sorted[:], in_=w_raw[:].rearrange("p (m j) -> p j m", j=PACK)
        )
        by_items = [c == 0 or c == N_CHUNKS - 1 for c in range(N_CHUNKS)]
        step1[0] = multiply(sums1_pool, quantise(z1_grouped[0]), by_items[0])

        def regroup_z1(c):
            grouped_z1 = grouped_pool.tile([P, CHUNK, FEATS, PACK], BF16, align_bytes=64)
            for b in range(CHUNK):
                regroup(nc.scalar.copy, grouped_z1, z1_tiles[c], b)
            z1_grouped[c] = grouped_z1

        for r in range(N_CHUNKS + 1):
            if r >= 1:
                step2[r - 1] = multiply(
                    sums2_pool, quantise(z2_grouped[r - 1]), by_items[r - 1]
                )
            if r < N_CHUNKS:
                if r + 2 < N_CHUNKS and not by_items[r]:
                    regroup_z1(r + 2)
                z2 = results.tile([P, CHUNK, NODES], F32, name="result", align_bytes=DMA_ALIGN)
                grouped_z2 = grouped_pool.tile([P, CHUNK, FEATS, PACK], BF16, align_bytes=64)
                for i in range(CHUNK):
                    combine(z2, step1[r], z0_tiles[r], i, by_items[r])
                for b in range(CHUNK):
                    regroup(nc.scalar.copy, grouped_z2, z2, b)
                z2_grouped[r] = grouped_z2
                nc.sync.dma_start(out=by_partition(out_0, r), in_=z2[:])
            if r + 1 < N_CHUNKS:
                step1[r + 1] = multiply(
                    sums1_pool, quantise(z1_grouped[r + 1]), by_items[r + 1]
                )
            if r + 2 < N_CHUNKS and by_items[r]:
                regroup_z1(r + 2)
            if r >= 1:
                z3 = results.tile([P, CHUNK, NODES], F32, name="result", align_bytes=DMA_ALIGN)
                last = r == N_CHUNKS
                for i in range(CHUNK):
                    combine(z3, step2[r - 1], z1_tiles[r - 1], i, by_items[r - 1])
                    if last:
                        (nc.scalar if i % 2 == 0 else nc.sync).dma_start(
                            out=by_partition(out_1, r - 1)[:, i : i + 1, :], in_=z3[:, i : i + 1, :]
                        )
                if not last:
                    nc.scalar.dma_start(out=by_partition(out_1, r - 1), in_=z3[:])
